import numpy as np
import ml_dtypes


def mxq(x, axis, fmt="e4m3"):
    dtype, down = {"e4m3": (ml_dtypes.float8_e4m3fn, 7), "e5m2": (ml_dtypes.float8_e5m2, 14)}[fmt]
    v = np.moveaxis(np.asarray(x, np.float32).astype(ml_dtypes.bfloat16).astype(np.float64), axis, -1)
    blocks = v.reshape(v.shape[:-1] + (-1, 32))
    amax = np.abs(blocks).max(-1, keepdims=True)
    byte = np.maximum(np.where(amax > 0, np.frexp(amax)[1] - 1 + 127, 0) - down, 1)
    scale = np.exp2(byte - 127.0)
    codes = (blocks / scale).astype(np.float32).astype(dtype).astype(np.float64)
    return np.moveaxis((codes * scale).reshape(v.shape), -1, axis)


WIDE = False


def mx_kscale(k):
    if not WIDE:
        return np.ones(k)
    levels = np.array([10, -10, 5, -5, 0])
    a = np.random.permutation(np.resize(levels, k // 512 * 4)).reshape(k // 512, 4)
    idx = np.arange(k)
    return np.exp2(a[idx // 512, idx % 128 // 32])


BF16 = ml_dtypes.bfloat16


def bf(x):
    return np.asarray(x, np.float32).astype(BF16)


def f64(x):
    return np.asarray(x).astype(np.float64)


M, SP, H, FF, NH = 4096, 3072, 512, 2560, 8
EPS = 1.1920929e-07


def rms_norm(x, w):
    var = np.mean(np.square(x), axis=-1, keepdims=True)
    return x * (1.0 / np.sqrt(var + EPS)) * w


def setup_inputs():
    s = mx_kscale(H)
    return {"x": bf(np.random.standard_normal((M, H))),
            "W_qkv": bf(np.random.standard_normal((2, H, 3 * H)) * 1.25 / np.sqrt(H) / s[None, :, None]),
            "ln1": bf((1.0 + 0.1 * np.random.standard_normal((2, H))) * s)}


def reference(x, W_qkv, ln1):
    x, W_qkv, ln1 = f64(x), f64(W_qkv), f64(ln1)
    h0 = rms_norm(x[:SP], ln1[0])
    h1 = rms_norm(x[SP:], ln1[1])
    y0 = mxq(h0, 1, "e4m3") @ mxq(W_qkv[0], 0, "e4m3")
    y1 = mxq(h1, 1, "e4m3") @ mxq(W_qkv[1], 0, "e4m3")
    return np.concatenate([y0, y1], axis=0)

@@ -1,0 +1,171 @@
+from contextlib import ExitStack
+
+import concourse.mybir as mybir
+from concourse.masks import make_identity
+
+F32 = mybir.dt.float32
+BF16 = mybir.dt.bfloat16
+U32 = mybir.dt.uint32
+U8 = mybir.dt.uint8
+FP8X4 = mybir.dt.float8_e4m3fn_x4
+ALU = mybir.AluOpType
+ACT = mybir.ActivationFunctionType
+
+ROWS = 4096
+SPLIT = 3072
+H = 512
+N_OUT = 1536
+EPS = 1.1920929e-07
+
+P = 128
+PACK = 4
+N_PASS = 512
+N_CHUNKS = N_OUT // N_PASS
+GROUP = 4
+GROUP_ROWS = P * GROUP
+N_GROUPS = ROWS // GROUP_ROWS
+MODELS = 2
+
+FLOPS = 2 * ROWS * H * N_OUT
+
+
+def tile_twomodelblockrouted_pa_t_kernel(tc, x, W_qkv, ln1, out):
+    nc = tc.nc
+    with ExitStack() as ctx:
+        const = ctx.enter_context(tc.tile_pool(name="const", bufs=1))
+        x_pool = ctx.enter_context(tc.tile_pool(name="x_pool", bufs=N_GROUPS))
+        w_in = ctx.enter_context(tc.tile_pool(name="w_in", bufs=MODELS))
+        w_stage = ctx.enter_context(tc.tile_pool(name="w_stage", bufs=2))
+        w_keep = ctx.enter_context(tc.tile_pool(name="w_keep", bufs=MODELS * N_CHUNKS))
+        stats = ctx.enter_context(tc.tile_pool(name="stats", bufs=3))
+        work = ctx.enter_context(tc.tile_pool(name="work", bufs=4))
+        out_pool = ctx.enter_context(tc.tile_pool(name="out_pool", bufs=6))
+        psum_t = ctx.enter_context(tc.psum_pool(name="psum_t", bufs=2))
+        psum_acc = ctx.enter_context(tc.psum_pool(name="psum_acc", bufs=6))
+
+        gain_rows = const.tile([P, P], BF16)
+        nc.vector.memset(gain_rows[:], 0.0)
+        nc.sync.dma_start(
+            out=gain_rows[0 : MODELS * PACK, :],
+            in_=ln1.rearrange("m (t p) -> (m t) p", p=P),
+        )
+
+        def load_x(g):
+            x_g = x_pool.tile([P, GROUP, H], BF16)
+            rows = x[g * GROUP_ROWS : (g + 1) * GROUP_ROWS, :]
+            nc.sync.dma_start(out=x_g[:], in_=rows.rearrange("(p j) k -> p j k", j=GROUP))
+            return x_g
+
+        def load_w(m):
+            w_raw = w_in.tile([P, PACK, N_OUT], BF16)
+            nc.sync.dma_start(out=w_raw[:], in_=W_qkv[m].rearrange("(t p) n -> p t n", p=P))
+            return w_raw
+
+        x_tiles = [load_x(0)]
+        w_raws = [load_w(0)]
+        x_tiles.extend([load_x(g) for g in range(1, 4)])
+        w_raws.append(load_w(1))
+        x_tiles.extend([load_x(g) for g in range(4, N_GROUPS)])
+
+        ident = const.tile([P, P], F32)
+        make_identity(nc, ident[:])
+
+        gain_rows_f = const.tile([P, P], F32)
+        nc.vector.tensor_copy(out=gain_rows_f[:], in_=gain_rows[:])
+        gains_ps = psum_t.tile([P, PACK, P], F32, tag="xt")
+        nc.tensor.transpose(gains_ps[:, 0, :], gain_rows_f[:], ident[:])
+        gains = const.tile([P, MODELS * PACK], F32)
+        nc.vector.tensor_copy(out=gains[:], in_=gains_ps[:, 0, 0 : MODELS * PACK])
+
+        def quantise_weights(m):
+            chunks = []
+            for c in range(N_CHUNKS):
+                cols = slice(c * N_PASS, (c + 1) * N_PASS)
+                w_grouped = w_stage.tile([P, N_PASS, PACK], BF16, align_bytes=64)
+                nc.vector.tensor_copy(
+                    out=w_grouped[:].rearrange("p (c i) t -> p c t i", i=4),
+                    in_=w_raws[m][:, :, cols].rearrange("p t (c i) -> p c t i", i=4),
+                )
+                w_codes = w_keep.tile([P, N_PASS], U32, align_bytes=64)
+                w_scales = w_keep.tile([P, N_PASS], U8, align_bytes=64)
+                nc.vector.quantize_mx(
+                    out=w_codes[:].bitcast(FP8X4),
+                    scales=w_scales[:],
+                    in_=w_grouped[:].rearrange("p n t -> p (n t)"),
+                )
+                chunks.append((w_codes, w_scales))
+            return chunks
+
+        def row_scales(g):
+            sumsq = stats.tile([P, GROUP], F32)
+            for j in range(GROUP):
+                squares = work.tile([P, H], BF16)
+                nc.scalar.activation(
+                    out=squares[:],
+                    in_=x_tiles[g][:, j, :],
+                    func=ACT.Square,
+                    accum_out=sumsq[:, j : j + 1],
+                )
+            meansq = stats.tile([P, GROUP], F32)
+            nc.vector.tensor_scalar(
+                out=meansq[:], in0=sumsq[:], scalar1=1.0 / H, scalar2=EPS, op0=ALU.mult, op1=ALU.add
+            )
+            rms = stats.tile([P, GROUP], F32)
+            nc.scalar.sqrt(rms[:], meansq[:])
+            rstd = stats.tile([P, GROUP], F32)
+            nc.vector.reciprocal(rstd[:], rms[:])
+            return rstd
+
+        def row_tile(g, j, rstd, m, weights):
+            xs = work.tile([P, H], F32)
+            nc.vector.tensor_scalar(
+                out=xs[:], in0=x_tiles[g][:, j, :], scalar1=rstd[:, j : j + 1], scalar2=None, op0=ALU.mult
+            )
+            xt = psum_t.tile([P, PACK, P], F32, tag="xt")
+            for t in range(PACK):
+                nc.tensor.transpose(xt[:, t, :], xs[:, t * P : (t + 1) * P], ident[:])
+            h_grouped = work.tile([P, P, PACK], BF16, align_bytes=64)
+            nc.vector.tensor_tensor(
+                out=h_grouped[:],
+                in0=xt[:].rearrange("p t r -> p r t"),
+                in1=gains[:, m * PACK : (m + 1) * PACK].unsqueeze(1).to_broadcast([P, P, PACK]),
+                op=ALU.mult,
+            )
+            h_codes = work.tile([P, P], U32, align_bytes=64)
+            h_scales = work.tile([P, P], U8, align_bytes=64)
+            nc.vector.quantize_mx(
+                out=h_codes[:].bitcast(FP8X4),
+                scales=h_scales[:],
+                in_=h_grouped[:].rearrange("p r t -> p (r t)"),
+            )
+            result = out_pool.tile([P, N_OUT], F32)
+            for c in range(N_CHUNKS):
+                cols = slice(c * N_PASS, (c + 1) * N_PASS)
+                w_codes, w_scales = weights[c]
+                acc = psum_acc.tile([P, N_PASS], F32)
+                nc.tensor.matmul_mx(
+                    out=acc[:],
+                    lhsT=h_codes[:].bitcast(FP8X4),
+                    lhsT_scale=h_scales[:],
+                    rhs=w_codes[:].bitcast(FP8X4),
+                    rhs_scale=w_scales[:],
+                    start=True,
+                    stop=True,
+                )
+                if c < 2:
+                    nc.scalar.copy(out=result[:, cols], in_=acc[:])
+                else:
+                    nc.vector.tensor_copy(out=result[:, cols], in_=acc[:])
+            rows = out[g * GROUP_ROWS : (g + 1) * GROUP_ROWS, :]
+            nc.sync.dma_start(out=rows.rearrange("(p j) n -> p j n", j=GROUP)[:, j, :], in_=result[:])
+
+        weights = [quantise_weights(0), None]
+        rstds = [row_scales(0)]
+        for g in range(N_GROUPS):
+            if g + 1 < N_GROUPS:
+                rstds.append(row_scales(g + 1))
+            if g == 2:
+                weights[1] = quantise_weights(1)
+            m = 0 if g * GROUP_ROWS < SPLIT else 1
+            for j in range(GROUP):
+                row_tile(g, j, rstds[g], m, weights[m])

@@ -16,15 +16,26 @@ SPLIT = 3072
 H = 512
 N_OUT = 1536
 EPS = 1.1920929e-07
+MODELS = 2
 
 P = 128
 PACK = 4
 N_PASS = 512
 N_CHUNKS = N_OUT // N_PASS
+W_PIECE = 256
+W_PIECES = N_OUT // W_PIECE
 GROUP = 4
 GROUP_ROWS = P * GROUP
 N_GROUPS = ROWS // GROUP_ROWS
-MODELS = 2
+N_TILES = ROWS // P
+
+LAG_TRANSPOSE = 1
+LAG_GAINS = 2
+LAG_MULTIPLY = 3
+LAG_DRAIN = 4
+STATS_LEAD = 5
+W0_PER_STEP = 2
+W1_FIRST_STEP = 10
 
 FLOPS = 2 * ROWS * H * N_OUT
 
@@ -32,19 +43,27 @@ FLOPS = 2 * ROWS * H * N_OUT
 def tile_twomodelblockrouted_pa_t_kernel(tc, x, W_qkv, ln1, out):
     nc = tc.nc
     with ExitStack() as ctx:
+        ctx.enter_context(tc.manual_schedule())
         const = ctx.enter_context(tc.tile_pool(name="const", bufs=1))
         x_pool = ctx.enter_context(tc.tile_pool(name="x_pool", bufs=N_GROUPS))
         w_in = ctx.enter_context(tc.tile_pool(name="w_in", bufs=MODELS))
-        w_stage = ctx.enter_context(tc.tile_pool(name="w_stage", bufs=2))
-        w_keep = ctx.enter_context(tc.tile_pool(name="w_keep", bufs=MODELS * N_CHUNKS))
+        w_stage = ctx.enter_context(tc.tile_pool(name="w_stage", bufs=3))
+        w_keep = ctx.enter_context(tc.tile_pool(name="w_keep", bufs=MODELS))
         stats = ctx.enter_context(tc.tile_pool(name="stats", bufs=3))
-        work = ctx.enter_context(tc.tile_pool(name="work", bufs=4))
-        out_pool = ctx.enter_context(tc.tile_pool(name="out_pool", bufs=6))
+        work = ctx.enter_context(tc.tile_pool(name="work", bufs=3))
+        out_pool = ctx.enter_context(tc.tile_pool(name="out_pool", bufs=8))
         psum_t = ctx.enter_context(tc.psum_pool(name="psum_t", bufs=2))
-        psum_acc = ctx.enter_context(tc.psum_pool(name="psum_acc", bufs=6))
+        psum_acc = ctx.enter_context(tc.psum_pool(name="psum_acc", bufs=2 * N_CHUNKS))
 
         gain_rows = const.tile([P, P], BF16)
         nc.vector.memset(gain_rows[:], 0.0)
+        eps_col = const.tile([P, 1], F32)
+        nc.vector.memset(eps_col[:], EPS)
+        ident = const.tile([P, P], F32)
+        make_identity(nc, ident[:])
+        warm = const.tile([P, 1], F32)
+        nc.scalar.activation(out=warm[:], in_=eps_col[:], func=ACT.Sqrt)
+
         nc.sync.dma_start(
             out=gain_rows[0 : MODELS * PACK, :],
             in_=ln1.rearrange("m (t p) -> (m t) p", p=P),
@@ -67,105 +86,169 @@ def tile_twomodelblockrouted_pa_t_kernel(tc, x, W_qkv, ln1, out):
         w_raws.append(load_w(1))
         x_tiles.extend([load_x(g) for g in range(4, N_GROUPS)])
 
-        ident = const.tile([P, P], F32)
-        make_identity(nc, ident[:])
+        w_codes = []
+        w_scales = []
+        for m in range(MODELS):
+            codes = w_keep.tile([P, N_OUT], U32, align_bytes=64)
+            scales = w_keep.tile([P, N_OUT], U8, align_bytes=64)
+            w_codes.append(codes)
+            w_scales.append(scales)
+
+        def regroup_weights(m, piece):
+            cols = slice(piece * W_PIECE, (piece + 1) * W_PIECE)
+            w_grouped = w_stage.tile([P, W_PIECE, PACK], BF16, align_bytes=64)
+            nc.vector.tensor_copy(
+                out=w_grouped[:].rearrange("p (c i) t -> p c t i", i=4),
+                in_=w_raws[m][:, :, cols].rearrange("p t (c i) -> p c t i", i=4),
+            )
+            return w_grouped, cols
+
+        def quantise_weights(m, w_grouped, cols):
+            nc.vector.quantize_mx(
+                out=w_codes[m][:, cols].bitcast(FP8X4),
+                scales=w_scales[m][:, cols],
+                in_=w_grouped[:].rearrange("p n t -> p (n t)"),
+            )
+
+        sumsq = {}
+        rms = {}
+        rstd = {}
+        xs = {}
+        xt = {}
+        h_grouped = {}
+        h_codes = {}
+        h_scales = {}
+        acc = {}
+
+        def square_sum(i):
+            g, j = divmod(i, GROUP)
+            if j == 0:
+                sumsq_g = stats.tile([P, GROUP], F32)
+                sumsq[g] = sumsq_g
+            squares = work.tile([P, H], BF16)
+            nc.scalar.activation(
+                out=squares[:], in_=x_tiles[g][:, j, :], func=ACT.Square, accum_out=sumsq[g][:, j : j + 1]
+            )
+            if j == GROUP - 1:
+                rms_g = stats.tile([P, GROUP], F32)
+                nc.scalar.activation(
+                    out=rms_g[:], in_=sumsq[g][:], func=ACT.Sqrt, scale=1.0 / H, bias=eps_col[:]
+                )
+                rms[g] = rms_g
+
+        def invert_rms(g):
+            rstd_g = stats.tile([P, GROUP], F32)
+            nc.vector.reciprocal(rstd_g[:], rms[g][:])
+            rstd[g] = rstd_g
+
+        def scale_rows(i):
+            g, j = divmod(i, GROUP)
+            xs_i = work.tile([P, H], F32)
+            nc.vector.tensor_scalar(
+                out=xs_i[:], in0=x_tiles[g][:, j, :], scalar1=rstd[g][:, j : j + 1], scalar2=None, op0=ALU.mult
+            )
+            xs[i] = xs_i
+
+        def transpose_rows(i):
+            xt_i = psum_t.tile([P, PACK, P], F32)
+            for t in range(PACK):
+                nc.tensor.transpose(xt_i[:, t, :], xs[i][:, t * P : (t + 1) * P], ident[:])
+            xt[i] = xt_i
+
+        def apply_gains(i):
+            m = 0 if i * P < SPLIT else 1
+            grouped = work.tile([P, P, PACK], BF16, align_bytes=64)
+            nc.vector.tensor_tensor(
+                out=grouped[:],
+                in0=xt[i][:].rearrange("p t r -> p r t"),
+                in1=gains[:, m * PACK : (m + 1) * PACK].unsqueeze(1).to_broadcast([P, P, PACK]),
+                op=ALU.mult,
+            )
+            h_grouped[i] = grouped
+
+        def quantise_rows(i):
+            codes_i = work.tile([P, P], U32, align_bytes=64)
+            scales_i = work.tile([P, P], U8, align_bytes=64)
+            nc.vector.quantize_mx(
+                out=codes_i[:].bitcast(FP8X4),
+                scales=scales_i[:],
+                in_=h_grouped[i][:].rearrange("p r t -> p (r t)"),
+            )
+            h_codes[i] = codes_i
+            h_scales[i] = scales_i
+
+        def multiply(i):
+            m = 0 if i * P < SPLIT else 1
+            banks = []
+            for c in range(N_CHUNKS):
+                cols = slice(c * N_PASS, (c + 1) * N_PASS)
+                bank = psum_acc.tile([P, N_PASS], F32)
+                nc.tensor.matmul_mx(
+                    out=bank[:],
+                    lhsT=h_codes[i][:].bitcast(FP8X4),
+                    lhsT_scale=h_scales[i][:],
+                    rhs=w_codes[m][:, cols].bitcast(FP8X4),
+                    rhs_scale=w_scales[m][:, cols],
+                    start=True,
+                    stop=True,
+                )
+                banks.append(bank)
+            acc[i] = banks
+
+        def drain_and_store(i, vector_banks):
+            g, j = divmod(i, GROUP)
+            result = out_pool.tile([P, N_OUT], F32)
+            for c in range(N_CHUNKS):
+                cols = slice(c * N_PASS, (c + 1) * N_PASS)
+                if c < N_CHUNKS - vector_banks:
+                    nc.scalar.copy(out=result[:, cols], in_=acc[i][c][:])
+                else:
+                    nc.vector.tensor_copy(out=result[:, cols], in_=acc[i][c][:])
+            rows = out[g * GROUP_ROWS : (g + 1) * GROUP_ROWS, :]
+            nc.sync.dma_start(out=rows.rearrange("(p j) n -> p j n", j=GROUP)[:, j, :], in_=result[:])
+
+        for i in range(STATS_LEAD):
+            square_sum(i)
 
         gain_rows_f = const.tile([P, P], F32)
         nc.vector.tensor_copy(out=gain_rows_f[:], in_=gain_rows[:])
-        gains_ps = psum_t.tile([P, PACK, P], F32, tag="xt")
+        gains_ps = psum_t.tile([P, PACK, P], F32, tag="xt_i")
         nc.tensor.transpose(gains_ps[:, 0, :], gain_rows_f[:], ident[:])
         gains = const.tile([P, MODELS * PACK], F32)
         nc.vector.tensor_copy(out=gains[:], in_=gains_ps[:, 0, 0 : MODELS * PACK])
 
-        def quantise_weights(m):
-            chunks = []
-            for c in range(N_CHUNKS):
-                cols = slice(c * N_PASS, (c + 1) * N_PASS)
-                w_grouped = w_stage.tile([P, N_PASS, PACK], BF16, align_bytes=64)
-                nc.vector.tensor_copy(
-                    out=w_grouped[:].rearrange("p (c i) t -> p c t i", i=4),
-                    in_=w_raws[m][:, :, cols].rearrange("p t (c i) -> p c t i", i=4),
-                )
-                w_codes = w_keep.tile([P, N_PASS], U32, align_bytes=64)
-                w_scales = w_keep.tile([P, N_PASS], U8, align_bytes=64)
-                nc.vector.quantize_mx(
-                    out=w_codes[:].bitcast(FP8X4),
-                    scales=w_scales[:],
-                    in_=w_grouped[:].rearrange("p n t -> p (n t)"),
-                )
-                chunks.append((w_codes, w_scales))
-            return chunks
+        invert_rms(0)
 
-        def row_scales(g):
-            sumsq = stats.tile([P, GROUP], F32)
-            for j in range(GROUP):
-                squares = work.tile([P, H], BF16)
-                nc.scalar.activation(
-                    out=squares[:],
-                    in_=x_tiles[g][:, j, :],
-                    func=ACT.Square,
-                    accum_out=sumsq[:, j : j + 1],
-                )
-            meansq = stats.tile([P, GROUP], F32)
-            nc.vector.tensor_scalar(
-                out=meansq[:], in0=sumsq[:], scalar1=1.0 / H, scalar2=EPS, op0=ALU.mult, op1=ALU.add
-            )
-            rms = stats.tile([P, GROUP], F32)
-            nc.scalar.sqrt(rms[:], meansq[:])
-            rstd = stats.tile([P, GROUP], F32)
-            nc.vector.reciprocal(rstd[:], rms[:])
-            return rstd
+        def live(i):
+            return 0 <= i < N_TILES
 
-        def row_tile(g, j, rstd, m, weights):
-            xs = work.tile([P, H], F32)
-            nc.vector.tensor_scalar(
-                out=xs[:], in0=x_tiles[g][:, j, :], scalar1=rstd[:, j : j + 1], scalar2=None, op0=ALU.mult
-            )
-            xt = psum_t.tile([P, PACK, P], F32, tag="xt")
-            for t in range(PACK):
-                nc.tensor.transpose(xt[:, t, :], xs[:, t * P : (t + 1) * P], ident[:])
-            h_grouped = work.tile([P, P, PACK], BF16, align_bytes=64)
-            nc.vector.tensor_tensor(
-                out=h_grouped[:],
-                in0=xt[:].rearrange("p t r -> p r t"),
-                in1=gains[:, m * PACK : (m + 1) * PACK].unsqueeze(1).to_broadcast([P, P, PACK]),
-                op=ALU.mult,
-            )
-            h_codes = work.tile([P, P], U32, align_bytes=64)
-            h_scales = work.tile([P, P], U8, align_bytes=64)
-            nc.vector.quantize_mx(
-                out=h_codes[:].bitcast(FP8X4),
-                scales=h_scales[:],
-                in_=h_grouped[:].rearrange("p r t -> p (r t)"),
-            )
-            result = out_pool.tile([P, N_OUT], F32)
-            for c in range(N_CHUNKS):
-                cols = slice(c * N_PASS, (c + 1) * N_PASS)
-                w_codes, w_scales = weights[c]
-                acc = psum_acc.tile([P, N_PASS], F32)
-                nc.tensor.matmul_mx(
-                    out=acc[:],
-                    lhsT=h_codes[:].bitcast(FP8X4),
-                    lhsT_scale=h_scales[:],
-                    rhs=w_codes[:].bitcast(FP8X4),
-                    rhs_scale=w_scales[:],
-                    start=True,
-                    stop=True,
-                )
-                if c < 2:
-                    nc.scalar.copy(out=result[:, cols], in_=acc[:])
-                else:
-                    nc.vector.tensor_copy(out=result[:, cols], in_=acc[:])
-            rows = out[g * GROUP_ROWS : (g + 1) * GROUP_ROWS, :]
-            nc.sync.dma_start(out=rows.rearrange("(p j) n -> p j n", j=GROUP)[:, j, :], in_=result[:])
+        def weight_pieces(s):
+            if s * W0_PER_STEP < W_PIECES:
+                return [(0, s * W0_PER_STEP + n) for n in range(W0_PER_STEP)]
+            if 0 <= s - W1_FIRST_STEP < W_PIECES:
+                return [(1, s - W1_FIRST_STEP)]
+            return []
 
-        weights = [quantise_weights(0), None]
-        rstds = [row_scales(0)]
-        for g in range(N_GROUPS):
-            if g + 1 < N_GROUPS:
-                rstds.append(row_scales(g + 1))
-            if g == 2:
-                weights[1] = quantise_weights(1)
-            m = 0 if g * GROUP_ROWS < SPLIT else 1
-            for j in range(GROUP):
-                row_tile(g, j, rstds[g], m, weights[m])
+        assert W_PIECES <= W0_PER_STEP * LAG_MULTIPLY
+
+        for s in range(N_TILES + LAG_DRAIN):
+            pieces = weight_pieces(s)
+            if live(s - LAG_MULTIPLY):
+                quantise_rows(s - LAG_MULTIPLY)
+            if live(s - LAG_TRANSPOSE):
+                transpose_rows(s - LAG_TRANSPOSE)
+            if live(s - LAG_MULTIPLY):
+                multiply(s - LAG_MULTIPLY)
+            if live(s):
+                scale_rows(s)
+            regrouped = [(m, regroup_weights(m, piece)) for m, piece in pieces]
+            if live(s - LAG_GAINS):
+                apply_gains(s - LAG_GAINS)
+            for m, (w_grouped, cols) in regrouped:
+                quantise_weights(m, w_grouped, cols)
+            if live(s - LAG_DRAIN):
+                drain_and_store(s - LAG_DRAIN, 0 if pieces else 1)
+            if live(s + 1) and (s + 1) % GROUP == 0:
+                invert_rms((s + 1) // GROUP)
+            if live(s + STATS_LEAD):
+                square_sum(s + STATS_LEAD)

@@ -33,9 +33,10 @@ LAG_TRANSPOSE = 1
 LAG_GAINS = 2
 LAG_MULTIPLY = 3
 LAG_DRAIN = 4
-STATS_LEAD = 5
-W0_PER_STEP = 2
-W1_FIRST_STEP = 10
+STATS_LEAD = 12
+W_HALVES = 2
+W_HALF = N_OUT // W_HALVES
+W1_FIRST_STEP = N_TILES - STATS_LEAD
 
 FLOPS = 2 * ROWS * H * N_OUT
 
@@ -46,11 +47,11 @@ def tile_twomodelblockrouted_pa_t_kernel(tc, x, W_qkv, ln1, out):
         ctx.enter_context(tc.manual_schedule())
         const = ctx.enter_context(tc.tile_pool(name="const", bufs=1))
         x_pool = ctx.enter_context(tc.tile_pool(name="x_pool", bufs=N_GROUPS))
-        w_in = ctx.enter_context(tc.tile_pool(name="w_in", bufs=MODELS))
+        w_in = ctx.enter_context(tc.tile_pool(name="w_in", bufs=MODELS * W_HALVES))
         w_stage = ctx.enter_context(tc.tile_pool(name="w_stage", bufs=3))
         w_keep = ctx.enter_context(tc.tile_pool(name="w_keep", bufs=MODELS))
-        stats = ctx.enter_context(tc.tile_pool(name="stats", bufs=3))
-        work = ctx.enter_context(tc.tile_pool(name="work", bufs=3))
+        stats = ctx.enter_context(tc.tile_pool(name="stats", bufs=N_GROUPS))
+        work = ctx.enter_context(tc.tile_pool(name="work", bufs=4))
         out_pool = ctx.enter_context(tc.tile_pool(name="out_pool", bufs=8))
         psum_t = ctx.enter_context(tc.psum_pool(name="psum_t", bufs=2))
         psum_acc = ctx.enter_context(tc.psum_pool(name="psum_acc", bufs=2 * N_CHUNKS))
@@ -64,26 +65,29 @@ def tile_twomodelblockrouted_pa_t_kernel(tc, x, W_qkv, ln1, out):
         warm = const.tile([P, 1], F32)
         nc.scalar.activation(out=warm[:], in_=eps_col[:], func=ACT.Sqrt)
 
-        nc.sync.dma_start(
-            out=gain_rows[0 : MODELS * PACK, :],
-            in_=ln1.rearrange("m (t p) -> (m t) p", p=P),
-        )
-
         def load_x(g):
             x_g = x_pool.tile([P, GROUP, H], BF16)
             rows = x[g * GROUP_ROWS : (g + 1) * GROUP_ROWS, :]
             nc.sync.dma_start(out=x_g[:], in_=rows.rearrange("(p j) k -> p j k", j=GROUP))
             return x_g
 
-        def load_w(m):
-            w_raw = w_in.tile([P, PACK, N_OUT], BF16)
-            nc.sync.dma_start(out=w_raw[:], in_=W_qkv[m].rearrange("(t p) n -> p t n", p=P))
+        def load_w(m, half):
+            w_raw = w_in.tile([P, PACK, W_HALF], BF16)
+            cols = slice(half * W_HALF, (half + 1) * W_HALF)
+            nc.sync.dma_start(out=w_raw[:], in_=W_qkv[m, :, cols].rearrange("(t p) n -> p t n", p=P))
             return w_raw
 
+        w_raws = {}
+        w_raws[(0, 0)] = load_w(0, 0)
         x_tiles = [load_x(0)]
-        w_raws = [load_w(0)]
+        nc.sync.dma_start(
+            out=gain_rows[0 : MODELS * PACK, :],
+            in_=ln1.rearrange("m (t p) -> (m t) p", p=P),
+        )
+        w_raws[(0, 1)] = load_w(0, 1)
         x_tiles.extend([load_x(g) for g in range(1, 4)])
-        w_raws.append(load_w(1))
+        w_raws[(1, 0)] = load_w(1, 0)
+        w_raws[(1, 1)] = load_w(1, 1)
         x_tiles.extend([load_x(g) for g in range(4, N_GROUPS)])
 
         w_codes = []
@@ -96,10 +100,12 @@ def tile_twomodelblockrouted_pa_t_kernel(tc, x, W_qkv, ln1, out):
 
         def regroup_weights(m, piece):
             cols = slice(piece * W_PIECE, (piece + 1) * W_PIECE)
+            half, piece_in_half = divmod(piece, W_PIECES // W_HALVES)
+            cols_in_half = slice(piece_in_half * W_PIECE, (piece_in_half + 1) * W_PIECE)
             w_grouped = w_stage.tile([P, W_PIECE, PACK], BF16, align_bytes=64)
             nc.vector.tensor_copy(
                 out=w_grouped[:].rearrange("p (c i) t -> p c t i", i=4),
-                in_=w_raws[m][:, :, cols].rearrange("p t (c i) -> p c t i", i=4),
+                in_=w_raws[(m, half)][:, :, cols_in_half].rearrange("p t (c i) -> p c t i", i=4),
             )
             return w_grouped, cols
 
@@ -144,8 +150,13 @@ def tile_twomodelblockrouted_pa_t_kernel(tc, x, W_qkv, ln1, out):
         def scale_rows(i):
             g, j = divmod(i, GROUP)
             xs_i = work.tile([P, H], F32)
-            nc.vector.tensor_scalar(
-                out=xs_i[:], in0=x_tiles[g][:, j, :], scalar1=rstd[g][:, j : j + 1], scalar2=None, op0=ALU.mult
+            nc.gpsimd.tensor_scalar(
+                out=xs_i[:],
+                in0=x_tiles[g][:, j, :],
+                scalar1=rstd[g][:, j : j + 1],
+                scalar2=0.0,
+                op0=ALU.mult,
+                op1=ALU.add,
             )
             xs[i] = xs_i
 
@@ -210,6 +221,13 @@ def tile_twomodelblockrouted_pa_t_kernel(tc, x, W_qkv, ln1, out):
         for i in range(STATS_LEAD):
             square_sum(i)
 
+        waiting = regroup_weights(0, 0)
+        for piece in range(1, W_PIECES):
+            copied = regroup_weights(0, piece)
+            quantise_weights(0, waiting[0], waiting[1])
+            waiting = copied
+        quantise_weights(0, waiting[0], waiting[1])
+
         gain_rows_f = const.tile([P, P], F32)
         nc.vector.tensor_copy(out=gain_rows_f[:], in_=gain_rows[:])
         gains_ps = psum_t.tile([P, PACK, P], F32, tag="xt_i")
@@ -223,13 +241,9 @@ def tile_twomodelblockrouted_pa_t_kernel(tc, x, W_qkv, ln1, out):
             return 0 <= i < N_TILES
 
         def weight_pieces(s):
-            if s * W0_PER_STEP < W_PIECES:
-                return [(0, s * W0_PER_STEP + n) for n in range(W0_PER_STEP)]
             if 0 <= s - W1_FIRST_STEP < W_PIECES:
                 return [(1, s - W1_FIRST_STEP)]
             return []
-
-        assert W_PIECES <= W0_PER_STEP * LAG_MULTIPLY
 
         for s in range(N_TILES + LAG_DRAIN):
             pieces = weight_pieces(s)
@@ -247,7 +261,13 @@ def tile_twomodelblockrouted_pa_t_kernel(tc, x, W_qkv, ln1, out):
             for m, (w_grouped, cols) in regrouped:
                 quantise_weights(m, w_grouped, cols)
             if live(s - LAG_DRAIN):
-                drain_and_store(s - LAG_DRAIN, 0 if pieces else 1)
+                if pieces:
+                    vector_banks = 0
+                elif live(s + STATS_LEAD):
+                    vector_banks = 1 + s % 2
+                else:
+                    vector_banks = 1
+                drain_and_store(s - LAG_DRAIN, vector_banks)
             if live(s + 1) and (s + 1) % GROUP == 0:
                 invert_rms((s + 1) // GROUP)
             if live(s + STATS_LEAD):

@@ -33,10 +33,9 @@ LAG_TRANSPOSE = 1
 LAG_GAINS = 2
 LAG_MULTIPLY = 3
 LAG_DRAIN = 4
-STATS_LEAD = 12
-W_HALVES = 2
-W_HALF = N_OUT // W_HALVES
-W1_FIRST_STEP = N_TILES - STATS_LEAD
+RSTD_AFTER_PIECE = 3
+STATS_LEAD = 8
+W1_FIRST_STEP = 21
 
 FLOPS = 2 * ROWS * H * N_OUT
 
@@ -47,7 +46,7 @@ def tile_twomodelblockrouted_pa_t_kernel(tc, x, W_qkv, ln1, out):
         ctx.enter_context(tc.manual_schedule())
         const = ctx.enter_context(tc.tile_pool(name="const", bufs=1))
         x_pool = ctx.enter_context(tc.tile_pool(name="x_pool", bufs=N_GROUPS))
-        w_in = ctx.enter_context(tc.tile_pool(name="w_in", bufs=MODELS * W_HALVES))
+        w_in = ctx.enter_context(tc.tile_pool(name="w_in", bufs=MODELS))
         w_stage = ctx.enter_context(tc.tile_pool(name="w_stage", bufs=3))
         w_keep = ctx.enter_context(tc.tile_pool(name="w_keep", bufs=MODELS))
         stats = ctx.enter_context(tc.tile_pool(name="stats", bufs=N_GROUPS))
@@ -56,8 +55,9 @@ def tile_twomodelblockrouted_pa_t_kernel(tc, x, W_qkv, ln1, out):
         psum_t = ctx.enter_context(tc.psum_pool(name="psum_t", bufs=2))
         psum_acc = ctx.enter_context(tc.psum_pool(name="psum_acc", bufs=2 * N_CHUNKS))
 
-        gain_rows = const.tile([P, P], BF16)
-        nc.vector.memset(gain_rows[:], 0.0)
+        gain_raw = const.tile([P, MODELS, PACK], BF16)
+        nc.scalar.dma_start(out=gain_raw[:], in_=ln1.rearrange("m (p t) -> p m t", t=PACK))
+
         eps_col = const.tile([P, 1], F32)
         nc.vector.memset(eps_col[:], EPS)
         ident = const.tile([P, P], F32)
@@ -71,23 +71,14 @@ def tile_twomodelblockrouted_pa_t_kernel(tc, x, W_qkv, ln1, out):
             nc.sync.dma_start(out=x_g[:], in_=rows.rearrange("(p j) k -> p j k", j=GROUP))
             return x_g
 
-        def load_w(m, half):
-            w_raw = w_in.tile([P, PACK, W_HALF], BF16)
-            cols = slice(half * W_HALF, (half + 1) * W_HALF)
-            nc.sync.dma_start(out=w_raw[:], in_=W_qkv[m, :, cols].rearrange("(t p) n -> p t n", p=P))
+        def load_w(m):
+            w_raw = w_in.tile([P, PACK, N_OUT], BF16)
+            nc.sync.dma_start(out=w_raw[:], in_=W_qkv[m].rearrange("(p t) n -> p t n", t=PACK))
             return w_raw
 
-        w_raws = {}
-        w_raws[(0, 0)] = load_w(0, 0)
-        x_tiles = [load_x(0)]
-        nc.sync.dma_start(
-            out=gain_rows[0 : MODELS * PACK, :],
-            in_=ln1.rearrange("m (t p) -> (m t) p", p=P),
-        )
-        w_raws[(0, 1)] = load_w(0, 1)
-        x_tiles.extend([load_x(g) for g in range(1, 4)])
-        w_raws[(1, 0)] = load_w(1, 0)
-        w_raws[(1, 1)] = load_w(1, 1)
+        w_raws = [load_w(0)]
+        x_tiles = [load_x(g) for g in range(4)]
+        w_raws.append(load_w(1))
         x_tiles.extend([load_x(g) for g in range(4, N_GROUPS)])
 
         w_codes = []
@@ -100,12 +91,10 @@ def tile_twomodelblockrouted_pa_t_kernel(tc, x, W_qkv, ln1, out):
 
         def regroup_weights(m, piece):
             cols = slice(piece * W_PIECE, (piece + 1) * W_PIECE)
-            half, piece_in_half = divmod(piece, W_PIECES // W_HALVES)
-            cols_in_half = slice(piece_in_half * W_PIECE, (piece_in_half + 1) * W_PIECE)
             w_grouped = w_stage.tile([P, W_PIECE, PACK], BF16, align_bytes=64)
             nc.vector.tensor_copy(
                 out=w_grouped[:].rearrange("p (c i) t -> p c t i", i=4),
-                in_=w_raws[(m, half)][:, :, cols_in_half].rearrange("p t (c i) -> p c t i", i=4),
+                in_=w_raws[m][:, :, cols].rearrange("p t (c i) -> p c t i", i=4),
             )
             return w_grouped, cols
 
@@ -149,10 +138,10 @@ def tile_twomodelblockrouted_pa_t_kernel(tc, x, W_qkv, ln1, out):
 
         def scale_rows(i):
             g, j = divmod(i, GROUP)
-            xs_i = work.tile([P, H], F32)
+            xs_i = work.tile([P, PACK, P], F32)
             nc.gpsimd.tensor_scalar(
                 out=xs_i[:],
-                in0=x_tiles[g][:, j, :],
+                in0=x_tiles[g][:, j, :].rearrange("p (q t) -> p t q", t=PACK),
                 scalar1=rstd[g][:, j : j + 1],
                 scalar2=0.0,
                 op0=ALU.mult,
@@ -163,7 +152,7 @@ def tile_twomodelblockrouted_pa_t_kernel(tc, x, W_qkv, ln1, out):
         def transpose_rows(i):
             xt_i = psum_t.tile([P, PACK, P], F32)
             for t in range(PACK):
-                nc.tensor.transpose(xt_i[:, t, :], xs[i][:, t * P : (t + 1) * P], ident[:])
+                nc.tensor.transpose(xt_i[:, t, :], xs[i][:, t, :], ident[:])
             xt[i] = xt_i
 
         def apply_gains(i):
@@ -221,21 +210,17 @@ def tile_twomodelblockrouted_pa_t_kernel(tc, x, W_qkv, ln1, out):
         for i in range(STATS_LEAD):
             square_sum(i)
 
+        gains = const.tile([P, MODELS * PACK], F32)
+        nc.vector.tensor_copy(out=gains[:], in_=gain_raw[:].rearrange("p m t -> p (m t)"))
+
         waiting = regroup_weights(0, 0)
         for piece in range(1, W_PIECES):
             copied = regroup_weights(0, piece)
             quantise_weights(0, waiting[0], waiting[1])
             waiting = copied
+            if piece == RSTD_AFTER_PIECE:
+                invert_rms(0)
         quantise_weights(0, waiting[0], waiting[1])
-
-        gain_rows_f = const.tile([P, P], F32)
-        nc.vector.tensor_copy(out=gain_rows_f[:], in_=gain_rows[:])
-        gains_ps = psum_t.tile([P, PACK, P], F32, tag="xt_i")
-        nc.tensor.transpose(gains_ps[:, 0, :], gain_rows_f[:], ident[:])
-        gains = const.tile([P, MODELS * PACK], F32)
-        nc.vector.tensor_copy(out=gains[:], in_=gains_ps[:, 0, 0 : MODELS * PACK])
-
-        invert_rms(0)
 
         def live(i):
             return 0 <= i < N_TILES

@@ -19,6 +19,7 @@ EPS = 1.1920929e-07
 MODELS = 2
 
 P = 128
+PAIRS = 2
 PACK = 4
 N_PASS = 512
 N_CHUNKS = N_OUT // N_PASS
@@ -30,12 +31,15 @@ N_GROUPS = ROWS // GROUP_ROWS
 N_TILES = ROWS // P
 
 LAG_TRANSPOSE = 1
-LAG_GAINS = 2
+LAG_GROUP = 2
 LAG_MULTIPLY = 3
 LAG_DRAIN = 4
-RSTD_AFTER_PIECE = 3
-STATS_LEAD = 8
-W1_FIRST_STEP = 21
+STATS_LEAD = 10
+VECTOR_TILES = GROUP
+W0_STEPS = {0: [0, 1], 1: [2, 3], 2: [4, 5]}
+W0_SCALAR_PIECE = 5
+W1_STRIDE = 3
+W1_LAST_STEP = SPLIT // P + LAG_MULTIPLY - 1
 
 FLOPS = 2 * ROWS * H * N_OUT
 
@@ -51,15 +55,17 @@ def tile_twomodelblockrouted_pa_t_kernel(tc, x, W_qkv, ln1, out):
         w_keep = ctx.enter_context(tc.tile_pool(name="w_keep", bufs=MODELS))
         stats = ctx.enter_context(tc.tile_pool(name="stats", bufs=N_GROUPS))
         work = ctx.enter_context(tc.tile_pool(name="work", bufs=4))
-        out_pool = ctx.enter_context(tc.tile_pool(name="out_pool", bufs=8))
+        out_pool = ctx.enter_context(tc.tile_pool(name="out_pool", bufs=10))
         psum_t = ctx.enter_context(tc.psum_pool(name="psum_t", bufs=2))
         psum_acc = ctx.enter_context(tc.psum_pool(name="psum_acc", bufs=2 * N_CHUNKS))
 
-        gain_raw = const.tile([P, MODELS, PACK], BF16)
-        nc.scalar.dma_start(out=gain_raw[:], in_=ln1.rearrange("m (p t) -> p m t", t=PACK))
+        gain_col = const.tile([P, MODELS, PACK], BF16)
+        nc.scalar.dma_start(out=gain_col[:], in_=ln1.rearrange("m (p t) -> p m t", t=PACK))
 
         eps_col = const.tile([P, 1], F32)
         nc.vector.memset(eps_col[:], EPS)
+        ident_bf = const.tile([P, P], BF16)
+        make_identity(nc, ident_bf[:])
         ident = const.tile([P, P], F32)
         make_identity(nc, ident[:])
         warm = const.tile([P, 1], F32)
@@ -76,8 +82,9 @@ def tile_twomodelblockrouted_pa_t_kernel(tc, x, W_qkv, ln1, out):
             nc.sync.dma_start(out=w_raw[:], in_=W_qkv[m].rearrange("(p t) n -> p t n", t=PACK))
             return w_raw
 
+        x_tiles = [load_x(0)]
         w_raws = [load_w(0)]
-        x_tiles = [load_x(g) for g in range(4)]
+        x_tiles.extend([load_x(g) for g in range(1, 4)])
         w_raws.append(load_w(1))
         x_tiles.extend([load_x(g) for g in range(4, N_GROUPS)])
 
@@ -91,11 +98,13 @@ def tile_twomodelblockrouted_pa_t_kernel(tc, x, W_qkv, ln1, out):
 
         def regroup_weights(m, piece):
             cols = slice(piece * W_PIECE, (piece + 1) * W_PIECE)
-            w_grouped = w_stage.tile([P, W_PIECE, PACK], BF16, align_bytes=64)
-            nc.vector.tensor_copy(
-                out=w_grouped[:].rearrange("p (c i) t -> p c t i", i=4),
-                in_=w_raws[m][:, :, cols].rearrange("p t (c i) -> p c t i", i=4),
-            )
+            source = w_raws[m][:, :, cols].rearrange("p t (c i) -> p c t i", i=4)
+            if m == 0 and piece == W0_SCALAR_PIECE:
+                w_grouped = w_stage.tile([P, W_PIECE, PACK], BF16, tag="by_scalar", bufs=1, align_bytes=64)
+                nc.scalar.copy(out=w_grouped[:].rearrange("p (c i) t -> p c t i", i=4), in_=source)
+            else:
+                w_grouped = w_stage.tile([P, W_PIECE, PACK], BF16, align_bytes=64)
+                nc.vector.tensor_copy(out=w_grouped[:].rearrange("p (c i) t -> p c t i", i=4), in_=source)
             return w_grouped, cols
 
         def quantise_weights(m, w_grouped, cols):
@@ -108,8 +117,8 @@ def tile_twomodelblockrouted_pa_t_kernel(tc, x, W_qkv, ln1, out):
         sumsq = {}
         rms = {}
         rstd = {}
-        xs = {}
-        xt = {}
+        scaled = {}
+        turned = {}
         h_grouped = {}
         h_codes = {}
         h_scales = {}
@@ -138,32 +147,56 @@ def tile_twomodelblockrouted_pa_t_kernel(tc, x, W_qkv, ln1, out):
 
         def scale_rows(i):
             g, j = divmod(i, GROUP)
-            xs_i = work.tile([P, PACK, P], F32)
-            nc.gpsimd.tensor_scalar(
-                out=xs_i[:],
-                in0=x_tiles[g][:, j, :].rearrange("p (q t) -> p t q", t=PACK),
-                scalar1=rstd[g][:, j : j + 1],
-                scalar2=0.0,
-                op0=ALU.mult,
-                op1=ALU.add,
-            )
-            xs[i] = xs_i
+            if i < VECTOR_TILES:
+                h_row = work.tile([P, H], BF16)
+                nc.vector.scalar_tensor_tensor(
+                    out=h_row[:].rearrange("p (n t) -> p n t", t=PACK),
+                    in0=x_tiles[g][:, j, :].rearrange("p (n t) -> p n t", t=PACK),
+                    scalar=rstd[g][:, j : j + 1],
+                    in1=spread[:].rearrange("p t n -> p n t"),
+                    op0=ALU.mult,
+                    op1=ALU.mult,
+                )
+                scaled[i] = h_row
+            else:
+                xs_i = work.tile([P, PACK, P], F32)
+                nc.gpsimd.tensor_scalar(
+                    out=xs_i[:],
+                    in0=x_tiles[g][:, j, :].rearrange("p (q t) -> p t q", t=PACK),
+                    scalar1=rstd[g][:, j : j + 1],
+                    scalar2=0.0,
+                    op0=ALU.mult,
+                    op1=ALU.add,
+                )
+                scaled[i] = xs_i
 
         def transpose_rows(i):
-            xt_i = psum_t.tile([P, PACK, P], F32)
-            for t in range(PACK):
-                nc.tensor.transpose(xt_i[:, t, :], xs[i][:, t, :], ident[:])
-            xt[i] = xt_i
+            if i < VECTOR_TILES:
+                turned_i = psum_t.tile([P, PAIRS, P], F32, tag="turned")
+                words = scaled[i][:].bitcast(F32)
+                for u in range(PAIRS):
+                    nc.tensor.transpose(turned_i[:, u, :], words[:, u : H // 2 : PAIRS], ident[:])
+            else:
+                turned_i = psum_t.tile([P, PACK, P], F32, tag="turned")
+                for t in range(PACK):
+                    nc.tensor.transpose(turned_i[:, t, :], scaled[i][:, t, :], ident[:])
+            turned[i] = turned_i
 
-        def apply_gains(i):
+        def group_rows(i):
             m = 0 if i * P < SPLIT else 1
             grouped = work.tile([P, P, PACK], BF16, align_bytes=64)
-            nc.vector.tensor_tensor(
-                out=grouped[:],
-                in0=xt[i][:].rearrange("p t r -> p r t"),
-                in1=gains[:, m * PACK : (m + 1) * PACK].unsqueeze(1).to_broadcast([P, P, PACK]),
-                op=ALU.mult,
-            )
+            if i < VECTOR_TILES:
+                words = grouped[:].rearrange("p r t -> p (r t)").bitcast(F32)
+                nc.vector.tensor_copy(
+                    out=words.rearrange("p (r u) -> p r u", u=PAIRS), in_=turned[i][:].rearrange("p u r -> p r u")
+                )
+            else:
+                nc.vector.tensor_tensor(
+                    out=grouped[:],
+                    in0=turned[i][:].rearrange("p t r -> p r t"),
+                    in1=gains[:, m * PACK : (m + 1) * PACK].unsqueeze(1).to_broadcast([P, P, PACK]),
+                    op=ALU.mult,
+                )
             h_grouped[i] = grouped
 
         def quantise_rows(i):
@@ -207,28 +240,31 @@ def tile_twomodelblockrouted_pa_t_kernel(tc, x, W_qkv, ln1, out):
             rows = out[g * GROUP_ROWS : (g + 1) * GROUP_ROWS, :]
             nc.sync.dma_start(out=rows.rearrange("(p j) n -> p j n", j=GROUP)[:, j, :], in_=result[:])
 
-        for i in range(STATS_LEAD):
+        spread = psum_acc.tile([P, PACK, P], F32, tag="bank")
+        for t in range(PACK):
+            nc.tensor.matmul(
+                spread[:, t, :],
+                lhsT=gain_col[:, 0, t : t + 1].to_broadcast([P, P]),
+                rhs=ident_bf[:],
+                start=True,
+                stop=True,
+            )
+
+        for i in range(GROUP):
             square_sum(i)
-
-        gains = const.tile([P, MODELS * PACK], F32)
-        nc.vector.tensor_copy(out=gains[:], in_=gain_raw[:].rearrange("p m t -> p (m t)"))
-
-        waiting = regroup_weights(0, 0)
-        for piece in range(1, W_PIECES):
-            copied = regroup_weights(0, piece)
-            quantise_weights(0, waiting[0], waiting[1])
-            waiting = copied
-            if piece == RSTD_AFTER_PIECE:
-                invert_rms(0)
-        quantise_weights(0, waiting[0], waiting[1])
+        by_scalar = regroup_weights(0, W0_SCALAR_PIECE)
+        for i in range(GROUP, STATS_LEAD):
+            square_sum(i)
+        invert_rms(0)
 
         def live(i):
             return 0 <= i < N_TILES
 
         def weight_pieces(s):
-            if 0 <= s - W1_FIRST_STEP < W_PIECES:
-                return [(1, s - W1_FIRST_STEP)]
-            return []
+            back, off_step = divmod(W1_LAST_STEP - s, W1_STRIDE)
+            if off_step == 0 and 0 <= back < W_PIECES:
+                return [(1, W_PIECES - 1 - back)]
+            return [(0, piece) for piece in W0_STEPS.get(s, [])]
 
         for s in range(N_TILES + LAG_DRAIN):
             pieces = weight_pieces(s)
@@ -238,22 +274,33 @@ def tile_twomodelblockrouted_pa_t_kernel(tc, x, W_qkv, ln1, out):
                 transpose_rows(s - LAG_TRANSPOSE)
             if live(s - LAG_MULTIPLY):
                 multiply(s - LAG_MULTIPLY)
+            regrouped = []
+            for m, piece in pieces:
+                if m == 0 and piece == W0_SCALAR_PIECE:
+                    regrouped.append((m, by_scalar))
+                else:
+                    regrouped.append((m, regroup_weights(m, piece)))
             if live(s):
                 scale_rows(s)
-            regrouped = [(m, regroup_weights(m, piece)) for m, piece in pieces]
-            if live(s - LAG_GAINS):
-                apply_gains(s - LAG_GAINS)
+            if s == VECTOR_TILES - 1:
+                gains = const.tile([P, MODELS * PACK], F32)
+                nc.vector.tensor_copy(out=gains[:], in_=gain_col[:].rearrange("p m t -> p (m t)"))
+            if live(s - LAG_GROUP):
+                group_rows(s - LAG_GROUP)
             for m, (w_grouped, cols) in regrouped:
                 quantise_weights(m, w_grouped, cols)
             if live(s - LAG_DRAIN):
                 if pieces:
                     vector_banks = 0
-                elif live(s + STATS_LEAD):
-                    vector_banks = 1 + s % 2
+                elif live(s + STATS_LEAD) and s % 3 == 0:
+                    vector_banks = 2
                 else:
                     vector_banks = 1
                 drain_and_store(s - LAG_DRAIN, vector_banks)
-            if live(s + 1) and (s + 1) % GROUP == 0:
-                invert_rms((s + 1) // GROUP)
+            if (s + 1) % GROUP == 0:
+                g = (s + 1) // GROUP
+                for ahead in [1, 2] if g == 1 else [g + 1]:
+                    if ahead < N_GROUPS:
+                        invert_rms(ahead)
             if live(s + STATS_LEAD):
                 square_sum(s + STATS_LEAD)

@@ -25,10 +25,12 @@ N_PASS = 512
 N_CHUNKS = N_OUT // N_PASS
 W_PIECE = 256
 W_PIECES = N_OUT // W_PIECE
-GROUP = 4
-GROUP_ROWS = P * GROUP
-N_GROUPS = ROWS // GROUP_ROWS
 N_TILES = ROWS // P
+GROUP = 4
+N_GROUPS = N_TILES // GROUP
+LOADS = [4, 4, 8, 8, 8]
+FIRST_SINGLES = 6
+STORE_TILES = 2
 
 LAG_TRANSPOSE = 1
 LAG_GROUP = 2
@@ -38,8 +40,7 @@ STATS_LEAD = 10
 VECTOR_TILES = GROUP
 W0_STEPS = {0: [0, 1], 1: [2, 3], 2: [4, 5]}
 W0_SCALAR_PIECE = 5
-W1_STRIDE = 3
-W1_LAST_STEP = SPLIT // P + LAG_MULTIPLY - 1
+W1_FIRST_STEP = SPLIT // P + LAG_MULTIPLY - W_PIECES
 
 FLOPS = 2 * ROWS * H * N_OUT
 
@@ -49,13 +50,13 @@ def tile_twomodelblockrouted_pa_t_kernel(tc, x, W_qkv, ln1, out):
     with ExitStack() as ctx:
         ctx.enter_context(tc.manual_schedule())
         const = ctx.enter_context(tc.tile_pool(name="const", bufs=1))
-        x_pool = ctx.enter_context(tc.tile_pool(name="x_pool", bufs=N_GROUPS))
+        x_pool = ctx.enter_context(tc.tile_pool(name="x_pool", bufs=1))
         w_in = ctx.enter_context(tc.tile_pool(name="w_in", bufs=MODELS))
         w_stage = ctx.enter_context(tc.tile_pool(name="w_stage", bufs=3))
         w_keep = ctx.enter_context(tc.tile_pool(name="w_keep", bufs=MODELS))
         stats = ctx.enter_context(tc.tile_pool(name="stats", bufs=N_GROUPS))
         work = ctx.enter_context(tc.tile_pool(name="work", bufs=4))
-        out_pool = ctx.enter_context(tc.tile_pool(name="out_pool", bufs=10))
+        out_pool = ctx.enter_context(tc.tile_pool(name="out_pool", bufs=8))
         psum_t = ctx.enter_context(tc.psum_pool(name="psum_t", bufs=2))
         psum_acc = ctx.enter_context(tc.psum_pool(name="psum_acc", bufs=2 * N_CHUNKS))
 
@@ -71,22 +72,31 @@ def tile_twomodelblockrouted_pa_t_kernel(tc, x, W_qkv, ln1, out):
         warm = const.tile([P, 1], F32)
         nc.scalar.activation(out=warm[:], in_=eps_col[:], func=ACT.Sqrt)
 
-        def load_x(g):
-            x_g = x_pool.tile([P, GROUP, H], BF16)
-            rows = x[g * GROUP_ROWS : (g + 1) * GROUP_ROWS, :]
-            nc.sync.dma_start(out=x_g[:], in_=rows.rearrange("(p j) k -> p j k", j=GROUP))
-            return x_g
+        x_of = {}
+        rows_of = {}
+
+        def load_x(number):
+            first = sum(LOADS[:number])
+            tiles = LOADS[number]
+            rows = slice(first * P, (first + tiles) * P)
+            x_load = x_pool.tile([P, tiles, H], BF16, tag="x_%d" % number)
+            nc.sync.dma_start(out=x_load[:], in_=x[rows, :].rearrange("(p j) k -> p j k", j=tiles))
+            for j in range(tiles):
+                x_of[first + j] = x_load[:, j, :]
+                rows_of[first + j] = (out[rows, :].rearrange("(p j) n -> p j n", j=tiles), j)
 
         def load_w(m):
             w_raw = w_in.tile([P, PACK, N_OUT], BF16)
             nc.sync.dma_start(out=w_raw[:], in_=W_qkv[m].rearrange("(p t) n -> p t n", t=PACK))
             return w_raw
 
-        x_tiles = [load_x(0)]
+        load_x(0)
         w_raws = [load_w(0)]
-        x_tiles.extend([load_x(g) for g in range(1, 4)])
+        load_x(1)
+        load_x(2)
         w_raws.append(load_w(1))
-        x_tiles.extend([load_x(g) for g in range(4, N_GROUPS)])
+        load_x(3)
+        load_x(4)
 
         w_codes = []
         w_scales = []
@@ -131,7 +141,7 @@ def tile_twomodelblockrouted_pa_t_kernel(tc, x, W_qkv, ln1, out):
                 sumsq[g] = sumsq_g
             squares = work.tile([P, H], BF16)
             nc.scalar.activation(
-                out=squares[:], in_=x_tiles[g][:, j, :], func=ACT.Square, accum_out=sumsq[g][:, j : j + 1]
+                out=squares[:], in_=x_of[i], func=ACT.Square, accum_out=sumsq[g][:, j : j + 1]
             )
             if j == GROUP - 1:
                 rms_g = stats.tile([P, GROUP], F32)
@@ -151,7 +161,7 @@ def tile_twomodelblockrouted_pa_t_kernel(tc, x, W_qkv, ln1, out):
                 h_row = work.tile([P, H], BF16)
                 nc.vector.scalar_tensor_tensor(
                     out=h_row[:].rearrange("p (n t) -> p n t", t=PACK),
-                    in0=x_tiles[g][:, j, :].rearrange("p (n t) -> p n t", t=PACK),
+                    in0=x_of[i].rearrange("p (n t) -> p n t", t=PACK),
                     scalar=rstd[g][:, j : j + 1],
                     in1=spread[:].rearrange("p t n -> p n t"),
                     op0=ALU.mult,
@@ -162,7 +172,7 @@ def tile_twomodelblockrouted_pa_t_kernel(tc, x, W_qkv, ln1, out):
                 xs_i = work.tile([P, PACK, P], F32)
                 nc.gpsimd.tensor_scalar(
                     out=xs_i[:],
-                    in0=x_tiles[g][:, j, :].rearrange("p (q t) -> p t q", t=PACK),
+                    in0=x_of[i].rearrange("p (q t) -> p t q", t=PACK),
                     scalar1=rstd[g][:, j : j + 1],
                     scalar2=0.0,
                     op0=ALU.mult,
@@ -228,17 +238,24 @@ def tile_twomodelblockrouted_pa_t_kernel(tc, x, W_qkv, ln1, out):
                 banks.append(bank)
             acc[i] = banks
 
+        results = {}
+
         def drain_and_store(i, vector_banks):
-            g, j = divmod(i, GROUP)
-            result = out_pool.tile([P, N_OUT], F32)
+            slot = 0 if i < FIRST_SINGLES else i % STORE_TILES
+            if slot == 0:
+                result = out_pool.tile([P, STORE_TILES, N_OUT], F32)
+            else:
+                result = results[i - slot]
+            results[i] = result
             for c in range(N_CHUNKS):
                 cols = slice(c * N_PASS, (c + 1) * N_PASS)
                 if c < N_CHUNKS - vector_banks:
-                    nc.scalar.copy(out=result[:, cols], in_=acc[i][c][:])
+                    nc.scalar.copy(out=result[:, slot, cols], in_=acc[i][c][:])
                 else:
-                    nc.vector.tensor_copy(out=result[:, cols], in_=acc[i][c][:])
-            rows = out[g * GROUP_ROWS : (g + 1) * GROUP_ROWS, :]
-            nc.sync.dma_start(out=rows.rearrange("(p j) n -> p j n", j=GROUP)[:, j, :], in_=result[:])
+                    nc.vector.tensor_copy(out=result[:, slot, cols], in_=acc[i][c][:])
+            if i < FIRST_SINGLES or slot == STORE_TILES - 1:
+                rows, j = rows_of[i]
+                nc.sync.dma_start(out=rows[:, j - slot : j + 1, :], in_=result[:, 0 : slot + 1, :])
 
         spread = psum_acc.tile([P, PACK, P], F32, tag="bank")
         for t in range(PACK):
@@ -261,9 +278,8 @@ def tile_twomodelblockrouted_pa_t_kernel(tc, x, W_qkv, ln1, out):
             return 0 <= i < N_TILES
 
         def weight_pieces(s):
-            back, off_step = divmod(W1_LAST_STEP - s, W1_STRIDE)
-            if off_step == 0 and 0 <= back < W_PIECES:
-                return [(1, W_PIECES - 1 - back)]
+            if 0 <= s - W1_FIRST_STEP < W_PIECES:
+                return [(1, s - W1_FIRST_STEP)]
             return [(0, piece) for piece in W0_STEPS.get(s, [])]
 
         for s in range(N_TILES + LAG_DRAIN):

@@ -51,7 +51,7 @@ def tile_twomodelblockrouted_pa_t_kernel(tc, x, W_qkv, ln1, out):
         ctx.enter_context(tc.manual_schedule())
         const = ctx.enter_context(tc.tile_pool(name="const", bufs=1))
         x_pool = ctx.enter_context(tc.tile_pool(name="x_pool", bufs=1))
-        w_in = ctx.enter_context(tc.tile_pool(name="w_in", bufs=MODELS))
+        w_in = ctx.enter_context(tc.tile_pool(name="w_in", bufs=1))
         w_stage = ctx.enter_context(tc.tile_pool(name="w_stage", bufs=3))
         w_keep = ctx.enter_context(tc.tile_pool(name="w_keep", bufs=MODELS))
         stats = ctx.enter_context(tc.tile_pool(name="stats", bufs=N_GROUPS))
@@ -85,16 +85,22 @@ def tile_twomodelblockrouted_pa_t_kernel(tc, x, W_qkv, ln1, out):
                 x_of[first + j] = x_load[:, j, :]
                 rows_of[first + j] = (out[rows, :].rearrange("(p j) n -> p j n", j=tiles), j)
 
-        def load_w(m):
-            w_raw = w_in.tile([P, PACK, N_OUT], BF16)
-            nc.sync.dma_start(out=w_raw[:], in_=W_qkv[m].rearrange("(p t) n -> p t n", t=PACK))
-            return w_raw
+        w_of = {}
+
+        def load_w(m, first_piece, pieces):
+            width = pieces * W_PIECE
+            cols = slice(first_piece * W_PIECE, first_piece * W_PIECE + width)
+            w_raw = w_in.tile([P, PACK, width], BF16, tag="w_%d_%d" % (m, first_piece))
+            nc.sync.dma_start(out=w_raw[:], in_=W_qkv[m, :, cols].rearrange("(p t) n -> p t n", t=PACK))
+            for piece in range(pieces):
+                w_of[(m, first_piece + piece)] = w_raw[:, :, piece * W_PIECE : (piece + 1) * W_PIECE]
 
         load_x(0)
-        w_raws = [load_w(0)]
+        load_w(0, 0, W_PIECES // 2)
+        load_w(0, W_PIECES // 2, W_PIECES // 2)
         load_x(1)
         load_x(2)
-        w_raws.append(load_w(1))
+        load_w(1, 0, W_PIECES)
         load_x(3)
         load_x(4)
 
@@ -108,7 +114,7 @@ def tile_twomodelblockrouted_pa_t_kernel(tc, x, W_qkv, ln1, out):
 
         def regroup_weights(m, piece):
             cols = slice(piece * W_PIECE, (piece + 1) * W_PIECE)
-            source = w_raws[m][:, :, cols].rearrange("p t (c i) -> p c t i", i=4)
+            source = w_of[(m, piece)].rearrange("p t (c i) -> p c t i", i=4)
             if m == 0 and piece == W0_SCALAR_PIECE:
                 w_grouped = w_stage.tile([P, W_PIECE, PACK], BF16, tag="by_scalar", bufs=1, align_bytes=64)
                 nc.scalar.copy(out=w_grouped[:].rearrange("p (c i) t -> p c t i", i=4), in_=source)
@@ -272,7 +278,6 @@ def tile_twomodelblockrouted_pa_t_kernel(tc, x, W_qkv, ln1, out):
         by_scalar = regroup_weights(0, W0_SCALAR_PIECE)
         for i in range(GROUP, STATS_LEAD):
             square_sum(i)
-        invert_rms(0)
 
         def live(i):
             return 0 <= i < N_TILES
@@ -296,6 +301,8 @@ def tile_twomodelblockrouted_pa_t_kernel(tc, x, W_qkv, ln1, out):
                     regrouped.append((m, by_scalar))
                 else:
                     regrouped.append((m, regroup_weights(m, piece)))
+            if s == 0:
+                invert_rms(0)
             if live(s):
                 scale_rows(s)
             if s == VECTOR_TILES - 1:
@@ -308,7 +315,7 @@ def tile_twomodelblockrouted_pa_t_kernel(tc, x, W_qkv, ln1, out):
             if live(s - LAG_DRAIN):
                 if pieces:
                     vector_banks = 0
-                elif live(s + STATS_LEAD) and s % 3 == 0:
+                elif live(s + STATS_LEAD) and s % 2 == 0:
                     vector_banks = 2
                 else:
                     vector_banks = 1

from contextlib import ExitStack

import concourse.mybir as mybir
from concourse.masks import make_identity

F32 = mybir.dt.float32
BF16 = mybir.dt.bfloat16
U32 = mybir.dt.uint32
U8 = mybir.dt.uint8
FP8X4 = mybir.dt.float8_e4m3fn_x4
ALU = mybir.AluOpType
ACT = mybir.ActivationFunctionType

ROWS = 4096
SPLIT = 3072
H = 512
N_OUT = 1536
EPS = 1.1920929e-07
MODELS = 2

P = 128
PAIRS = 2
PACK = 4
N_PASS = 512
N_CHUNKS = N_OUT // N_PASS
W_PIECE = 256
W_PIECES = N_OUT // W_PIECE
N_TILES = ROWS // P
GROUP = 4
N_GROUPS = N_TILES // GROUP
LOADS = [4, 4, 8, 8, 8]
FIRST_SINGLES = 6
STORE_TILES = 2

LAG_TRANSPOSE = 1
LAG_GROUP = 2
LAG_MULTIPLY = 3
LAG_DRAIN = 4
STATS_LEAD = 10
VECTOR_TILES = GROUP
W0_STEPS = {0: [0, 1], 1: [2, 3], 2: [4, 5]}
W0_SCALAR_PIECE = 5
W1_FIRST_STEP = SPLIT // P + LAG_MULTIPLY - W_PIECES

FLOPS = 2 * ROWS * H * N_OUT


def tile_twomodelblockrouted_pa_t_kernel(tc, x, W_qkv, ln1, out):
    nc = tc.nc
    with ExitStack() as ctx:
        ctx.enter_context(tc.manual_schedule())
        const = ctx.enter_context(tc.tile_pool(name="const", bufs=1))
        x_pool = ctx.enter_context(tc.tile_pool(name="x_pool", bufs=1))
        w_in = ctx.enter_context(tc.tile_pool(name="w_in", bufs=1))
        w_stage = ctx.enter_context(tc.tile_pool(name="w_stage", bufs=3))
        w_keep = ctx.enter_context(tc.tile_pool(name="w_keep", bufs=MODELS))
        stats = ctx.enter_context(tc.tile_pool(name="stats", bufs=N_GROUPS))
        work = ctx.enter_context(tc.tile_pool(name="work", bufs=4))
        out_pool = ctx.enter_context(tc.tile_pool(name="out_pool", bufs=8))
        psum_t = ctx.enter_context(tc.psum_pool(name="psum_t", bufs=2))
        psum_acc = ctx.enter_context(tc.psum_pool(name="psum_acc", bufs=2 * N_CHUNKS))

        gain_col = const.tile([P, MODELS, PACK], BF16)
        nc.scalar.dma_start(out=gain_col[:], in_=ln1.rearrange("m (p t) -> p m t", t=PACK))

        eps_col = const.tile([P, 1], F32)
        nc.vector.memset(eps_col[:], EPS)
        ident_bf = const.tile([P, P], BF16)
        make_identity(nc, ident_bf[:])
        ident = const.tile([P, P], F32)
        make_identity(nc, ident[:])
        warm = const.tile([P, 1], F32)
        nc.scalar.activation(out=warm[:], in_=eps_col[:], func=ACT.Sqrt)

        x_of = {}
        rows_of = {}

        def load_x(number):
            first = sum(LOADS[:number])
            tiles = LOADS[number]
            rows = slice(first * P, (first + tiles) * P)
            x_load = x_pool.tile([P, tiles, H], BF16, tag="x_%d" % number)
            nc.sync.dma_start(out=x_load[:], in_=x[rows, :].rearrange("(p j) k -> p j k", j=tiles))
            for j in range(tiles):
                x_of[first + j] = x_load[:, j, :]
                rows_of[first + j] = (out[rows, :].rearrange("(p j) n -> p j n", j=tiles), j)

        w_of = {}

        def load_w(m, first_piece, pieces):
            width = pieces * W_PIECE
            cols = slice(first_piece * W_PIECE, first_piece * W_PIECE + width)
            w_raw = w_in.tile([P, PACK, width], BF16, tag="w_%d_%d" % (m, first_piece))
            nc.sync.dma_start(out=w_raw[:], in_=W_qkv[m, :, cols].rearrange("(p t) n -> p t n", t=PACK))
            for piece in range(pieces):
                w_of[(m, first_piece + piece)] = w_raw[:, :, piece * W_PIECE : (piece + 1) * W_PIECE]

        load_x(0)
        load_w(0, 0, W_PIECES // 2)
        load_w(0, W_PIECES // 2, W_PIECES // 2)
        load_x(1)
        load_x(2)
        load_w(1, 0, W_PIECES)
        load_x(3)
        load_x(4)

        w_codes = []
        w_scales = []
        for m in range(MODELS):
            codes = w_keep.tile([P, N_OUT], U32, align_bytes=64)
            scales = w_keep.tile([P, N_OUT], U8, align_bytes=64)
            w_codes.append(codes)
            w_scales.append(scales)

        def regroup_weights(m, piece):
            cols = slice(piece * W_PIECE, (piece + 1) * W_PIECE)
            source = w_of[(m, piece)].rearrange("p t (c i) -> p c t i", i=4)
            if m == 0 and piece == W0_SCALAR_PIECE:
                w_grouped = w_stage.tile([P, W_PIECE, PACK], BF16, tag="by_scalar", bufs=1, align_bytes=64)
                nc.scalar.copy(out=w_grouped[:].rearrange("p (c i) t -> p c t i", i=4), in_=source)
            else:
                w_grouped = w_stage.tile([P, W_PIECE, PACK], BF16, align_bytes=64)
                nc.vector.tensor_copy(out=w_grouped[:].rearrange("p (c i) t -> p c t i", i=4), in_=source)
            return w_grouped, cols

        def quantise_weights(m, w_grouped, cols):
            nc.vector.quantize_mx(
                out=w_codes[m][:, cols].bitcast(FP8X4),
                scales=w_scales[m][:, cols],
                in_=w_grouped[:].rearrange("p n t -> p (n t)"),
            )

        sumsq = {}
        rms = {}
        rstd = {}
        scaled = {}
        turned = {}
        h_grouped = {}
        h_codes = {}
        h_scales = {}
        acc = {}

        def square_sum(i):
            g, j = divmod(i, GROUP)
            if j == 0:
                sumsq_g = stats.tile([P, GROUP], F32)
                sumsq[g] = sumsq_g
            squares = work.tile([P, H], BF16)
            nc.scalar.activation(
                out=squares[:], in_=x_of[i], func=ACT.Square, accum_out=sumsq[g][:, j : j + 1]
            )
            if j == GROUP - 1:
                rms_g = stats.tile([P, GROUP], F32)
                nc.scalar.activation(
                    out=rms_g[:], in_=sumsq[g][:], func=ACT.Sqrt, scale=1.0 / H, bias=eps_col[:]
                )
                rms[g] = rms_g

        def invert_rms(g):
            rstd_g = stats.tile([P, GROUP], F32)
            nc.vector.reciprocal(rstd_g[:], rms[g][:])
            rstd[g] = rstd_g

        def scale_rows(i):
            g, j = divmod(i, GROUP)
            if i < VECTOR_TILES:
                h_row = work.tile([P, H], BF16)
                nc.vector.scalar_tensor_tensor(
                    out=h_row[:].rearrange("p (n t) -> p n t", t=PACK),
                    in0=x_of[i].rearrange("p (n t) -> p n t", t=PACK),
                    scalar=rstd[g][:, j : j + 1],
                    in1=spread[:].rearrange("p t n -> p n t"),
                    op0=ALU.mult,
                    op1=ALU.mult,
                )
                scaled[i] = h_row
            else:
                xs_i = work.tile([P, PACK, P], F32)
                nc.gpsimd.tensor_scalar(
                    out=xs_i[:],
                    in0=x_of[i].rearrange("p (q t) -> p t q", t=PACK),
                    scalar1=rstd[g][:, j : j + 1],
                    scalar2=0.0,
                    op0=ALU.mult,
                    op1=ALU.add,
                )
                scaled[i] = xs_i

        def transpose_rows(i):
            if i < VECTOR_TILES:
                turned_i = psum_t.tile([P, PAIRS, P], F32, tag="turned")
                words = scaled[i][:].bitcast(F32)
                for u in range(PAIRS):
                    nc.tensor.transpose(turned_i[:, u, :], words[:, u : H // 2 : PAIRS], ident[:])
            else:
                turned_i = psum_t.tile([P, PACK, P], F32, tag="turned")
                for t in range(PACK):
                    nc.tensor.transpose(turned_i[:, t, :], scaled[i][:, t, :], ident[:])
            turned[i] = turned_i

        def group_rows(i):
            m = 0 if i * P < SPLIT else 1
            grouped = work.tile([P, P, PACK], BF16, align_bytes=64)
            if i < VECTOR_TILES:
                words = grouped[:].rearrange("p r t -> p (r t)").bitcast(F32)
                nc.vector.tensor_copy(
                    out=words.rearrange("p (r u) -> p r u", u=PAIRS), in_=turned[i][:].rearrange("p u r -> p r u")
                )
            else:
                nc.vector.tensor_tensor(
                    out=grouped[:],
                    in0=turned[i][:].rearrange("p t r -> p r t"),
                    in1=gains[:, m * PACK : (m + 1) * PACK].unsqueeze(1).to_broadcast([P, P, PACK]),
                    op=ALU.mult,
                )
            h_grouped[i] = grouped

        def quantise_rows(i):
            codes_i = work.tile([P, P], U32, align_bytes=64)
            scales_i = work.tile([P, P], U8, align_bytes=64)
            nc.vector.quantize_mx(
                out=codes_i[:].bitcast(FP8X4),
                scales=scales_i[:],
                in_=h_grouped[i][:].rearrange("p r t -> p (r t)"),
            )
            h_codes[i] = codes_i
            h_scales[i] = scales_i

        def multiply(i):
            m = 0 if i * P < SPLIT else 1
            banks = []
            for c in range(N_CHUNKS):
                cols = slice(c * N_PASS, (c + 1) * N_PASS)
                bank = psum_acc.tile([P, N_PASS], F32)
                nc.tensor.matmul_mx(
                    out=bank[:],
                    lhsT=h_codes[i][:].bitcast(FP8X4),
                    lhsT_scale=h_scales[i][:],
                    rhs=w_codes[m][:, cols].bitcast(FP8X4),
                    rhs_scale=w_scales[m][:, cols],
                    start=True,
                    stop=True,
                )
                banks.append(bank)
            acc[i] = banks

        results = {}

        def drain_and_store(i, vector_banks):
            slot = 0 if i < FIRST_SINGLES else i % STORE_TILES
            if slot == 0:
                result = out_pool.tile([P, STORE_TILES, N_OUT], F32)
            else:
                result = results[i - slot]
            results[i] = result
            for c in range(N_CHUNKS):
                cols = slice(c * N_PASS, (c + 1) * N_PASS)
                if c < N_CHUNKS - vector_banks:
                    nc.scalar.copy(out=result[:, slot, cols], in_=acc[i][c][:])
                else:
                    nc.vector.tensor_copy(out=result[:, slot, cols], in_=acc[i][c][:])
            if i < FIRST_SINGLES or slot == STORE_TILES - 1:
                rows, j = rows_of[i]
                nc.sync.dma_start(out=rows[:, j - slot : j + 1, :], in_=result[:, 0 : slot + 1, :])

        spread = psum_acc.tile([P, PACK, P], F32, tag="bank")
        for t in range(PACK):
            nc.tensor.matmul(
                spread[:, t, :],
                lhsT=gain_col[:, 0, t : t + 1].to_broadcast([P, P]),
                rhs=ident_bf[:],
                start=True,
                stop=True,
            )

        for i in range(GROUP):
            square_sum(i)
        by_scalar = regroup_weights(0, W0_SCALAR_PIECE)
        for i in range(GROUP, STATS_LEAD):
            square_sum(i)

        def live(i):
            return 0 <= i < N_TILES

        def weight_pieces(s):
            if 0 <= s - W1_FIRST_STEP < W_PIECES:
                return [(1, s - W1_FIRST_STEP)]
            return [(0, piece) for piece in W0_STEPS.get(s, [])]

        for s in range(N_TILES + LAG_DRAIN):
            pieces = weight_pieces(s)
            if live(s - LAG_MULTIPLY):
                quantise_rows(s - LAG_MULTIPLY)
            if live(s - LAG_TRANSPOSE):
                transpose_rows(s - LAG_TRANSPOSE)
            if live(s - LAG_MULTIPLY):
                multiply(s - LAG_MULTIPLY)
            regrouped = []
            for m, piece in pieces:
                if m == 0 and piece == W0_SCALAR_PIECE:
                    regrouped.append((m, by_scalar))
                else:
                    regrouped.append((m, regroup_weights(m, piece)))
            if s == 0:
                invert_rms(0)
            if live(s):
                scale_rows(s)
            if s == VECTOR_TILES - 1:
                gains = const.tile([P, MODELS * PACK], F32)
                nc.vector.tensor_copy(out=gains[:], in_=gain_col[:].rearrange("p m t -> p (m t)"))
            if live(s - LAG_GROUP):
                group_rows(s - LAG_GROUP)
            for m, (w_grouped, cols) in regrouped:
                quantise_weights(m, w_grouped, cols)
            if live(s - LAG_DRAIN):
                if pieces:
                    vector_banks = 0
                elif live(s + STATS_LEAD) and s % 2 == 0:
                    vector_banks = 2
                else:
                    vector_banks = 1
                drain_and_store(s - LAG_DRAIN, vector_banks)
            if (s + 1) % GROUP == 0:
                g = (s + 1) // GROUP
                for ahead in [1, 2] if g == 1 else [g + 1]:
                    if ahead < N_GROUPS:
                        invert_rms(ahead)
            if live(s + STATS_LEAD):
                square_sum(s + STATS_LEAD)
